import numpy as np
import ml_dtypes


def mxq(x, axis, fmt="e4m3"):
    dtype, down = {"e4m3": (ml_dtypes.float8_e4m3fn, 7), "e5m2": (ml_dtypes.float8_e5m2, 14)}[fmt]
    v = np.moveaxis(np.asarray(x, np.float32).astype(ml_dtypes.bfloat16).astype(np.float64), axis, -1)
    blocks = v.reshape(v.shape[:-1] + (-1, 32))
    amax = np.abs(blocks).max(-1, keepdims=True)
    byte = np.maximum(np.where(amax > 0, np.frexp(amax)[1] - 1 + 127, 0) - down, 1)
    scale = np.exp2(byte - 127.0)
    codes = (blocks / scale).astype(np.float32).astype(dtype).astype(np.float64)
    return np.moveaxis((codes * scale).reshape(v.shape), -1, axis)


WIDE = False


def mx_kscale(k):
    if not WIDE:
        return np.ones(k)
    levels = np.array([10, -10, 5, -5, 0])
    if k % 512:
        return np.exp2(np.random.permutation(np.resize(levels, k // 32))).repeat(32)
    a = np.empty((k // 512, 16))
    for p in range(k // 512):
        a[p, :8] = np.random.permutation(np.resize(levels, 8))
        for g in range(8):
            far = levels[np.abs(levels - a[p, g]) >= 10]
            a[p, g + 8] = far[np.random.randint(len(far))]
    return np.exp2(a.ravel()).repeat(32)


BF16 = ml_dtypes.bfloat16


def bf(x):
    return np.asarray(x, np.float32).astype(BF16)


def f64(x):
    return np.asarray(x).astype(np.float64)


B, N, HID, H, D = 2, 4096, 1024, 1, 128


def apply_rope(t, rope):
    freqs = rope[:, 0, :]
    cos = np.repeat(freqs[:, 0::2], 2, axis=-1)[None, None]
    sin = np.repeat(freqs[:, 1::2], 2, axis=-1)[None, None]
    tr = t.reshape(*t.shape[:-1], -1, 2)
    t_real, t_imag = tr[..., 0], tr[..., 1]
    t_rot = np.stack([-t_imag, t_real], axis=-1).reshape(t.shape)
    return t * cos + t_rot * sin


def setup_inputs():
    s = mx_kscale(HID)
    return {"x": bf(np.random.standard_normal((B, N, HID)) * s),
            "rope": bf(np.random.uniform(size=(N, 1, D))),
            "qkv_w": bf(np.random.standard_normal((HID, 3 * H * D)) * 1.5 / np.sqrt(HID) / s[:, None])}


def reference(x, rope, qkv_w):
    r = f64(rope)
    qkv = (mxq(f64(x), 2, "e4m3") @ mxq(f64(qkv_w), 0, "e4m3")).reshape(B, N, 3, H, D)
    q = np.transpose(qkv[:, :, 0], (0, 2, 1, 3))
    k = np.transpose(qkv[:, :, 1], (0, 2, 1, 3))
    v = np.transpose(qkv[:, :, 2], (0, 2, 1, 3))
    return apply_rope(q, r), apply_rope(k, r), v

@@ -1,0 +1,215 @@
+from contextlib import ExitStack
+
+import concourse.mybir as mybir
+from concourse.masks import make_identity
+
+F32 = mybir.dt.float32
+BF16 = mybir.dt.bfloat16
+U32 = mybir.dt.uint32
+U8 = mybir.dt.uint8
+FP8X4 = mybir.dt.float8_e4m3fn_x4
+ALU = mybir.AluOpType
+ACT = mybir.ActivationFunctionType
+
+P = 128
+B, N, HID, D = 2, 4096, 1024, 128
+FLOPS = 2 * B * N * HID * 3 * D
+
+ROWS_PP = N // P
+SU_T = 8
+U_T = 4
+N_SU = B * ROWS_PP // SU_T
+N_U = N_SU * SU_T // U_T
+NXS = 4
+
+
+def tile_attention_pa_t_kernel(tc, x, rope, qkv_w, out_0, out_1, out_2):
+    nc = tc.nc
+    x_v = x.rearrange("b (p t) k -> b p t k", t=ROWS_PP)
+    rope_v = rope.rearrange("(p t) o d -> p t (o d)", t=ROWS_PP)
+    o_v = [o.rearrange("b h (p t) d -> (b h) p t d", t=ROWS_PP) for o in (out_0, out_1, out_2)]
+
+    with ExitStack() as ctx:
+        const = ctx.enter_context(tc.tile_pool(name="const", bufs=1))
+        xpool = ctx.enter_context(tc.tile_pool(name="xpool", bufs=NXS))
+        gpool = ctx.enter_context(tc.tile_pool(name="gpool", bufs=2))
+        cpool = ctx.enter_context(tc.tile_pool(name="cpool", bufs=2))
+        m1pool = ctx.enter_context(tc.tile_pool(name="m1pool", bufs=3))
+        m2pool = ctx.enter_context(tc.tile_pool(name="m2pool", bufs=2))
+        vopool = ctx.enter_context(tc.tile_pool(name="vopool", bufs=3))
+        tpool = ctx.enter_context(tc.psum_pool(name="tpool", bufs=4))
+        qkpool = ctx.enter_context(tc.psum_pool(name="qkpool", bufs=3))
+        vpool = ctx.enter_context(tc.psum_pool(name="vpool", bufs=1))
+        ctx.enter_context(tc.manual_schedule())
+
+        ident = const.tile([P, P], F32, name="ident")
+        wraw = const.tile([P, 2, 4, 3 * D], BF16, name="wraw")
+        wg_qk = const.tile([P, 2, 2 * D, 4], BF16, name="wg_qk", align_bytes=64)
+        wg_v = const.tile([P, 2, D, 4], BF16, name="wg_v", align_bytes=64)
+        wc_qk = const.tile([P, 2 * 2 * D], U32, name="wc_qk", align_bytes=64)
+        ws_qk = const.tile([P, 2 * 2 * D], U8, name="ws_qk", align_bytes=64)
+        wc_v = const.tile([P, 2 * D], U32, name="wc_v", align_bytes=64)
+        ws_v = const.tile([P, 2 * D], U8, name="ws_v", align_bytes=64)
+        rope_sb = const.tile([P, ROWS_PP, D], BF16, name="rope_sb")
+        rope2 = const.tile([P, ROWS_PP, D], BF16, name="rope2")
+
+        xs, tps, grps, cods, scls, qks, vbs, m1s, m2s, vos = {}, {}, {}, {}, {}, {}, {}, {}, {}, {}
+
+        def where(u):
+            k = u // 2
+            return k, u % 2, k % 2, k // 2
+
+        def load_x(k, lo, hi):
+            if lo == 0:
+                xs[k] = xpool.tile([P, SU_T, HID], BF16, name="xs")
+            b, s = k % 2, k // 2
+            nc.sync.dma_start(out=xs[k][:, lo:hi, :], in_=x_v[b, :, SU_T * s + lo : SU_T * s + hi, :])
+
+        def load_rope(lo, hi):
+            nc.sync.dma_start(out=rope_sb[:, lo:hi, :], in_=rope_v[:, lo:hi, :])
+
+        def prep_rope2(s):
+            src = rope_sb[:, SU_T * s : SU_T * (s + 1), :].rearrange("p t (j e) -> p t j e", e=2)
+            dst = rope2[:, SU_T * s : SU_T * (s + 1), :].rearrange("p t (j e) -> p t j e", e=2)
+            nc.scalar.activation(out=dst[:, :, :, 0:1], in_=src[:, :, :, 1:2], func=ACT.Copy, scale=-1.0)
+            nc.scalar.copy(out=dst[:, :, :, 1:2], in_=src[:, :, :, 0:1])
+
+        def prep_w():
+            for g in range(2):
+                nc.vector.tensor_copy(out=wg_qk[:, g, :, :], in_=wraw[:, g, :, 0 : 2 * D].rearrange("p t c -> p c t"))
+            for g in range(2):
+                nc.vector.tensor_copy(out=wg_v[:, g, :, :], in_=wraw[:, g, :, 2 * D : 3 * D].rearrange("p t c -> p c t"))
+            nc.vector.quantize_mx(out=wc_qk[:].bitcast(FP8X4), scales=ws_qk[:], in_=wg_qk[:].rearrange("p g c t -> p (g c t)"))
+            nc.vector.quantize_mx(out=wc_v[:].bitcast(FP8X4), scales=ws_v[:], in_=wg_v[:].rearrange("p g c t -> p (g c t)"))
+
+        def transposes(u):
+            k, half, b, s = where(u)
+            tps[u] = []
+            for tt in range(U_T):
+                tp = tpool.tile([P, 4, P], F32, name="tp")
+                xf = xs[k][:, U_T * half + tt, :].bitcast(F32)
+                for i in range(4):
+                    nc.tensor.transpose(out=tp[:, i, :], in_=xf[:, 2 * P * (i // 2) + i % 2 : 2 * P * (i // 2 + 1) : 2], identity=ident[:])
+                tps[u].append(tp)
+
+        def copies(u):
+            grp = gpool.tile([P, U_T, HID], BF16, name="grp", align_bytes=64)
+            grps[u] = grp
+            for tt in range(U_T):
+                nc.scalar.copy(
+                    out=grp[:, tt, :].bitcast(F32).rearrange("p (g r w) -> p g r w", g=2, w=2),
+                    in_=tps[u][tt][:].rearrange("p (g w) r -> p g r w", w=2),
+                )
+
+        def quantise(u):
+            cod = cpool.tile([P, U_T * 2 * P], U32, name="cod", align_bytes=64)
+            scl = cpool.tile([P, U_T * 2 * P], U8, name="scl", align_bytes=64)
+            cods[u], scls[u] = cod, scl
+            nc.vector.quantize_mx(out=cod[:].bitcast(FP8X4), scales=scl[:], in_=grps[u][:].rearrange("p t k -> p (t k)"))
+
+        def mx(u):
+            cod, scl = cods[u], scls[u]
+            qks[u] = []
+            for h in range(2):
+                qk = qkpool.tile([P, 2, 2 * D], F32, name="qk")
+                qks[u].append(qk)
+                for j in range(2):
+                    for g in range(2):
+                        col = (2 * (2 * h + j) + g) * P
+                        nc.tensor.matmul_mx(
+                            out=qk[:, j, :],
+                            lhsT=cod[:, col : col + P].bitcast(FP8X4),
+                            lhsT_scale=scl[:, col : col + P],
+                            rhs=wc_qk[:, 2 * D * g : 2 * D * (g + 1)].bitcast(FP8X4),
+                            rhs_scale=ws_qk[:, 2 * D * g : 2 * D * (g + 1)],
+                            start=(g == 0),
+                            stop=(g == 1),
+                        )
+            vb = vpool.tile([P, U_T, D], F32, name="vb")
+            vbs[u] = vb
+            for tt in range(U_T):
+                for g in range(2):
+                    col = (2 * tt + g) * P
+                    nc.tensor.matmul_mx(
+                        out=vb[:, tt, :],
+                        lhsT=cod[:, col : col + P].bitcast(FP8X4),
+                        lhsT_scale=scl[:, col : col + P],
+                        rhs=wc_v[:, D * g : D * (g + 1)].bitcast(FP8X4),
+                        rhs_scale=ws_v[:, D * g : D * (g + 1)],
+                        start=(g == 0),
+                        stop=(g == 1),
+                    )
+
+        def v_out(u):
+            k, half, b, s = where(u)
+            if half == 0:
+                vos[k] = vopool.tile([P, SU_T, D], F32, name="vo")
+            nc.scalar.copy(out=vos[k][:, U_T * half : U_T * (half + 1), :], in_=vbs[u][:])
+
+        def products(u):
+            k, half, b, s = where(u)
+            if half == 0:
+                m1s[k] = m1pool.tile([P, 2, SU_T, D], F32, name="m1")
+            m2s[u] = m2pool.tile([P, 2, U_T, D], F32, name="m2")
+            shape = [P, 2, 2, D // 2, 2]
+            for h in range(2):
+                lt = U_T * half + 2 * h
+                t0 = SU_T * s + lt
+                pairs = qks[u][h][:].rearrange("p t (c j e) -> p t c j e", c=2, e=2)
+                for e, table, dst in (
+                    (0, rope_sb, m1s[k][:, :, lt : lt + 2, :]),
+                    (1, rope2, m2s[u][:, :, 2 * h : 2 * h + 2, :]),
+                ):
+                    nc.vector.tensor_tensor(
+                        out=dst.rearrange("p c t (j e) -> p t c j e", e=2),
+                        in0=pairs[:, :, :, :, e : e + 1].to_broadcast(shape),
+                        in1=table[:, t0 : t0 + 2, :].rearrange("p t (j e) -> p t j e", e=2).unsqueeze(2).to_broadcast(shape),
+                        op=ALU.mult,
+                    )
+
+        def add(u):
+            k, half, b, s = where(u)
+            dst = m1s[k][:, :, U_T * half : U_T * (half + 1), :]
+            nc.vector.tensor_tensor(out=dst, in0=dst, in1=m2s[u][:], op=ALU.add)
+
+        def stores(k):
+            b, s = k % 2, k // 2
+            rows = slice(SU_T * s, SU_T * (s + 1))
+            nc.sync.dma_start(out=o_v[0][b, :, rows, :], in_=m1s[k][:, 0, :, :])
+            nc.sync.dma_start(out=o_v[1][b, :, rows, :], in_=m1s[k][:, 1, :, :])
+            nc.sync.dma_start(out=o_v[2][b, :, rows, :], in_=vos[k][:])
+
+        make_identity(nc, ident[:])
+        load_x(0, 0, U_T)
+        nc.sync.dma_start(
+            out=wraw[:].rearrange("p g t c -> p g (t c)"),
+            in_=qkv_w.rearrange("(g p t) c -> p g (t c)", p=P, t=4),
+        )
+        load_rope(0, SU_T)
+        load_x(0, U_T, SU_T)
+        load_x(1, 0, SU_T)
+        load_rope(SU_T, ROWS_PP)
+        for k in range(2, NXS):
+            load_x(k, 0, SU_T)
+
+        for i in range(N_U + 1):
+            if i < N_U:
+                transposes(i)
+                copies(i)
+            if i >= 1:
+                mx(i - 1)
+            if i == 0:
+                prep_w()
+            if i < N_U:
+                quantise(i)
+            if i % 4 == 0 and i // 4 < ROWS_PP // SU_T:
+                prep_rope2(i // 4)
+            if i >= 1:
+                v_out(i - 1)
+                products(i - 1)
+                add(i - 1)
+                if (i - 1) % 2 == 1:
+                    k = (i - 1) // 2
+                    stores(k)
+                    if k + NXS < N_SU:
+                        load_x(k + NXS, 0, SU_T)

@@ -167,10 +167,11 @@ def tile_attention_pa_t_kernel(tc, x, rope, qkv_w, out_0, out_1, out_2):
                         op=ALU.mult,
                     )
 
-        def add(u):
+        def add(u, h, engine):
             k, half, b, s = where(u)
-            dst = m1s[k][:, :, U_T * half : U_T * (half + 1), :]
-            nc.vector.tensor_tensor(out=dst, in0=dst, in1=m2s[u][:], op=ALU.add)
+            lt = U_T * half + 2 * h
+            dst = m1s[k][:, :, lt : lt + 2, :]
+            engine.tensor_tensor(out=dst, in0=dst, in1=m2s[u][:, :, 2 * h : 2 * h + 2, :], op=ALU.add)
 
         def stores(k):
             b, s = k % 2, k // 2
@@ -192,11 +193,11 @@ def tile_attention_pa_t_kernel(tc, x, rope, qkv_w, out_0, out_1, out_2):
         for k in range(2, NXS):
             load_x(k, 0, SU_T)
 
-        for i in range(N_U + 1):
+        for i in range(N_U + 2):
             if i < N_U:
                 transposes(i)
                 copies(i)
-            if i >= 1:
+            if 1 <= i <= N_U:
                 mx(i - 1)
             if i == 0:
                 prep_w()
@@ -204,12 +205,14 @@ def tile_attention_pa_t_kernel(tc, x, rope, qkv_w, out_0, out_1, out_2):
                 quantise(i)
             if i % 4 == 0 and i // 4 < ROWS_PP // SU_T:
                 prep_rope2(i // 4)
-            if i >= 1:
-                v_out(i - 1)
-                products(i - 1)
-                add(i - 1)
-                if (i - 1) % 2 == 1:
-                    k = (i - 1) // 2
+            if i >= 2:
+                add(i - 2, 1, nc.vector)
+                if i % 2 == 1:
+                    k = (i - 2) // 2
                     stores(k)
                     if k + NXS < N_SU:
                         load_x(k + NXS, 0, SU_T)
+            if 1 <= i <= N_U:
+                v_out(i - 1)
+                products(i - 1)
+                add(i - 1, 0, nc.gpsimd)

@@ -82,22 +82,23 @@ def tile_attention_pa_t_kernel(tc, x, rope, qkv_w, out_0, out_1, out_2):
             nc.vector.quantize_mx(out=wc_qk[:].bitcast(FP8X4), scales=ws_qk[:], in_=wg_qk[:].rearrange("p g c t -> p (g c t)"))
             nc.vector.quantize_mx(out=wc_v[:].bitcast(FP8X4), scales=ws_v[:], in_=wg_v[:].rearrange("p g c t -> p (g c t)"))
 
-        def transposes(u):
+        def transposes(u, h):
             k, half, b, s = where(u)
-            tps[u] = []
-            for tt in range(U_T):
+            if h == 0:
+                tps[u] = []
+            for tt in range(2 * h, 2 * h + 2):
                 tp = tpool.tile([P, 4, P], F32, name="tp")
                 xf = xs[k][:, U_T * half + tt, :].bitcast(F32)
                 for i in range(4):
                     nc.tensor.transpose(out=tp[:, i, :], in_=xf[:, 2 * P * (i // 2) + i % 2 : 2 * P * (i // 2 + 1) : 2], identity=ident[:])
                 tps[u].append(tp)
 
-        def copies(u):
-            grp = gpool.tile([P, U_T, HID], BF16, name="grp", align_bytes=64)
-            grps[u] = grp
-            for tt in range(U_T):
+        def copies(u, h):
+            if h == 0:
+                grps[u] = gpool.tile([P, U_T, HID], BF16, name="grp", align_bytes=64)
+            for tt in range(2 * h, 2 * h + 2):
                 nc.scalar.copy(
-                    out=grp[:, tt, :].bitcast(F32).rearrange("p (g r w) -> p g r w", g=2, w=2),
+                    out=grps[u][:, tt, :].bitcast(F32).rearrange("p (g r w) -> p g r w", g=2, w=2),
                     in_=tps[u][tt][:].rearrange("p (g w) r -> p g r w", w=2),
                 )
 
@@ -107,31 +108,30 @@ def tile_attention_pa_t_kernel(tc, x, rope, qkv_w, out_0, out_1, out_2):
             cods[u], scls[u] = cod, scl
             nc.vector.quantize_mx(out=cod[:].bitcast(FP8X4), scales=scl[:], in_=grps[u][:].rearrange("p t k -> p (t k)"))
 
-        def mx(u):
+        def mx(u, h):
             cod, scl = cods[u], scls[u]
-            qks[u] = []
-            for h in range(2):
-                qk = qkpool.tile([P, 2, 2 * D], F32, name="qk")
-                qks[u].append(qk)
-                for j in range(2):
-                    for g in range(2):
-                        col = (2 * (2 * h + j) + g) * P
-                        nc.tensor.matmul_mx(
-                            out=qk[:, j, :],
-                            lhsT=cod[:, col : col + P].bitcast(FP8X4),
-                            lhsT_scale=scl[:, col : col + P],
-                            rhs=wc_qk[:, 2 * D * g : 2 * D * (g + 1)].bitcast(FP8X4),
-                            rhs_scale=ws_qk[:, 2 * D * g : 2 * D * (g + 1)],
-                            start=(g == 0),
-                            stop=(g == 1),
-                        )
-            vb = vpool.tile([P, U_T, D], F32, name="vb")
-            vbs[u] = vb
-            for tt in range(U_T):
+            if h == 0:
+                qks[u] = []
+                vbs[u] = vpool.tile([P, U_T, D], F32, name="vb")
+            qk = qkpool.tile([P, 2, 2 * D], F32, name="qk")
+            qks[u].append(qk)
+            for j in range(2):
+                for g in range(2):
+                    col = (2 * (2 * h + j) + g) * P
+                    nc.tensor.matmul_mx(
+                        out=qk[:, j, :],
+                        lhsT=cod[:, col : col + P].bitcast(FP8X4),
+                        lhsT_scale=scl[:, col : col + P],
+                        rhs=wc_qk[:, 2 * D * g : 2 * D * (g + 1)].bitcast(FP8X4),
+                        rhs_scale=ws_qk[:, 2 * D * g : 2 * D * (g + 1)],
+                        start=(g == 0),
+                        stop=(g == 1),
+                    )
+            for tt in range(2 * h, 2 * h + 2):
                 for g in range(2):
                     col = (2 * tt + g) * P
                     nc.tensor.matmul_mx(
-                        out=vb[:, tt, :],
+                        out=vbs[u][:, tt, :],
                         lhsT=cod[:, col : col + P].bitcast(FP8X4),
                         lhsT_scale=scl[:, col : col + P],
                         rhs=wc_v[:, D * g : D * (g + 1)].bitcast(FP8X4),
@@ -194,11 +194,12 @@ def tile_attention_pa_t_kernel(tc, x, rope, qkv_w, out_0, out_1, out_2):
             load_x(k, 0, SU_T)
 
         for i in range(N_U + 2):
-            if i < N_U:
-                transposes(i)
-                copies(i)
-            if 1 <= i <= N_U:
-                mx(i - 1)
+            for h in range(2):
+                if i < N_U:
+                    transposes(i, h)
+                    copies(i, h)
+                if 1 <= i <= N_U:
+                    mx(i - 1, h)
             if i == 0:
                 prep_w()
             if i < N_U:

@@ -33,7 +33,7 @@ def tile_attention_pa_t_kernel(tc, x, rope, qkv_w, out_0, out_1, out_2):
         const = ctx.enter_context(tc.tile_pool(name="const", bufs=1))
         xpool = ctx.enter_context(tc.tile_pool(name="xpool", bufs=NXS))
         gpool = ctx.enter_context(tc.tile_pool(name="gpool", bufs=2))
-        cpool = ctx.enter_context(tc.tile_pool(name="cpool", bufs=2))
+        cpool = ctx.enter_context(tc.tile_pool(name="cpool", bufs=3))
         m1pool = ctx.enter_context(tc.tile_pool(name="m1pool", bufs=3))
         m2pool = ctx.enter_context(tc.tile_pool(name="m2pool", bufs=2))
         vopool = ctx.enter_context(tc.tile_pool(name="vopool", bufs=3))
@@ -193,27 +193,27 @@ def tile_attention_pa_t_kernel(tc, x, rope, qkv_w, out_0, out_1, out_2):
         for k in range(2, NXS):
             load_x(k, 0, SU_T)
 
-        for i in range(N_U + 2):
+        for i in range(N_U + 3):
             for h in range(2):
                 if i < N_U:
                     transposes(i, h)
                     copies(i, h)
-                if 1 <= i <= N_U:
-                    mx(i - 1, h)
+                if 2 <= i < N_U + 2:
+                    mx(i - 2, h)
             if i == 0:
                 prep_w()
             if i < N_U:
                 quantise(i)
             if i % 4 == 0 and i // 4 < ROWS_PP // SU_T:
                 prep_rope2(i // 4)
-            if i >= 2:
-                add(i - 2, 1, nc.vector)
-                if i % 2 == 1:
-                    k = (i - 2) // 2
+            if i >= 3:
+                add(i - 3, 1, nc.vector)
+                if i % 2 == 0:
+                    k = (i - 3) // 2
                     stores(k)
                     if k + NXS < N_SU:
                         load_x(k + NXS, 0, SU_T)
-            if 1 <= i <= N_U:
-                v_out(i - 1)
-                products(i - 1)
-                add(i - 1, 0, nc.gpsimd)
+            if 2 <= i < N_U + 2:
+                v_out(i - 2)
+                products(i - 2)
+                add(i - 2, 0, nc.gpsimd)

@@ -17,9 +17,10 @@ FLOPS = 2 * B * N * HID * 3 * D
 
 ROWS_PP = N // P
 SU_T = 8
-U_T = 4
 N_SU = B * ROWS_PP // SU_T
-N_U = N_SU * SU_T // U_T
+R_T = 2
+N_R = N_SU * SU_T // R_T
+R_SU = SU_T // R_T
 NXS = 4
 
 
@@ -32,10 +33,11 @@ def tile_attention_pa_t_kernel(tc, x, rope, qkv_w, out_0, out_1, out_2):
     with ExitStack() as ctx:
         const = ctx.enter_context(tc.tile_pool(name="const", bufs=1))
         xpool = ctx.enter_context(tc.tile_pool(name="xpool", bufs=NXS))
-        gpool = ctx.enter_context(tc.tile_pool(name="gpool", bufs=2))
-        cpool = ctx.enter_context(tc.tile_pool(name="cpool", bufs=3))
-        m1pool = ctx.enter_context(tc.tile_pool(name="m1pool", bufs=3))
-        m2pool = ctx.enter_context(tc.tile_pool(name="m2pool", bufs=2))
+        gpool = ctx.enter_context(tc.tile_pool(name="gpool", bufs=4))
+        cpool = ctx.enter_context(tc.tile_pool(name="cpool", bufs=5))
+        opool = ctx.enter_context(tc.tile_pool(name="opool", bufs=3))
+        m1pool = ctx.enter_context(tc.tile_pool(name="m1pool", bufs=4))
+        m2pool = ctx.enter_context(tc.tile_pool(name="m2pool", bufs=4))
         vopool = ctx.enter_context(tc.tile_pool(name="vopool", bufs=3))
         tpool = ctx.enter_context(tc.psum_pool(name="tpool", bufs=4))
         qkpool = ctx.enter_context(tc.psum_pool(name="qkpool", bufs=3))
@@ -53,11 +55,11 @@ def tile_attention_pa_t_kernel(tc, x, rope, qkv_w, out_0, out_1, out_2):
         rope_sb = const.tile([P, ROWS_PP, D], BF16, name="rope_sb")
         rope2 = const.tile([P, ROWS_PP, D], BF16, name="rope2")
 
-        xs, tps, grps, cods, scls, qks, vbs, m1s, m2s, vos = {}, {}, {}, {}, {}, {}, {}, {}, {}, {}
+        xs, tps, grps, cods, scls, qks, vbs, m1s, m2s, outs, vos = {}, {}, {}, {}, {}, {}, {}, {}, {}, {}, {}
 
-        def where(u):
-            k = u // 2
-            return k, u % 2, k % 2, k // 2
+        def where(r):
+            k = r // R_SU
+            return k, R_T * (r % R_SU), k % 2, k // 2
 
         def load_x(k, lo, hi):
             if lo == 0:
@@ -82,44 +84,42 @@ def tile_attention_pa_t_kernel(tc, x, rope, qkv_w, out_0, out_1, out_2):
             nc.vector.quantize_mx(out=wc_qk[:].bitcast(FP8X4), scales=ws_qk[:], in_=wg_qk[:].rearrange("p g c t -> p (g c t)"))
             nc.vector.quantize_mx(out=wc_v[:].bitcast(FP8X4), scales=ws_v[:], in_=wg_v[:].rearrange("p g c t -> p (g c t)"))
 
-        def transposes(u, h):
-            k, half, b, s = where(u)
-            if h == 0:
-                tps[u] = []
-            for tt in range(2 * h, 2 * h + 2):
+        def transposes(r):
+            k, lt, b, s = where(r)
+            tps[r] = []
+            for tt in range(R_T):
                 tp = tpool.tile([P, 4, P], F32, name="tp")
-                xf = xs[k][:, U_T * half + tt, :].bitcast(F32)
+                xf = xs[k][:, lt + tt, :].bitcast(F32)
                 for i in range(4):
-                    nc.tensor.transpose(out=tp[:, i, :], in_=xf[:, 2 * P * (i // 2) + i % 2 : 2 * P * (i // 2 + 1) : 2], identity=ident[:])
-                tps[u].append(tp)
+                    words = slice(2 * P * (i // 2) + i % 2, 2 * P * (i // 2 + 1), 2)
+                    nc.tensor.transpose(out=tp[:, i, :], in_=xf[:, words], identity=ident[:])
+                tps[r].append(tp)
 
-        def copies(u, h):
-            if h == 0:
-                grps[u] = gpool.tile([P, U_T, HID], BF16, name="grp", align_bytes=64)
-            for tt in range(2 * h, 2 * h + 2):
+        def copies(r):
+            grps[r] = gpool.tile([P, R_T, HID], BF16, name="grp", align_bytes=64)
+            for tt in range(R_T):
                 nc.scalar.copy(
-                    out=grps[u][:, tt, :].bitcast(F32).rearrange("p (g r w) -> p g r w", g=2, w=2),
-                    in_=tps[u][tt][:].rearrange("p (g w) r -> p g r w", w=2),
+                    out=grps[r][:, tt, :].bitcast(F32).rearrange("p (g r w) -> p g r w", g=2, w=2),
+                    in_=tps[r][tt][:].rearrange("p (g w) r -> p g r w", w=2),
                 )
 
-        def quantise(u):
-            cod = cpool.tile([P, U_T * 2 * P], U32, name="cod", align_bytes=64)
-            scl = cpool.tile([P, U_T * 2 * P], U8, name="scl", align_bytes=64)
-            cods[u], scls[u] = cod, scl
-            nc.vector.quantize_mx(out=cod[:].bitcast(FP8X4), scales=scl[:], in_=grps[u][:].rearrange("p t k -> p (t k)"))
+        def quantise(r):
+            cod = cpool.tile([P, R_T * 2 * P], U32, name="cod", align_bytes=64)
+            scl = cpool.tile([P, R_T * 2 * P], U8, name="scl", align_bytes=64)
+            cods[r], scls[r] = cod, scl
+            nc.vector.quantize_mx(out=cod[:].bitcast(FP8X4), scales=scl[:], in_=grps[r][:].rearrange("p t k -> p (t k)"))
 
-        def mx(u, h):
-            cod, scl = cods[u], scls[u]
-            if h == 0:
-                qks[u] = []
-                vbs[u] = vpool.tile([P, U_T, D], F32, name="vb")
-            qk = qkpool.tile([P, 2, 2 * D], F32, name="qk")
-            qks[u].append(qk)
-            for j in range(2):
+        def mx(r):
+            cod, scl = cods[r], scls[r]
+            if r % 2 == 0:
+                vbs[r // 2] = vpool.tile([P, 2 * R_T, D], F32, name="vb")
+            qk = qkpool.tile([P, R_T, 2 * D], F32, name="qk")
+            qks[r] = qk
+            for tt in range(R_T):
                 for g in range(2):
-                    col = (2 * (2 * h + j) + g) * P
+                    col = (2 * tt + g) * P
                     nc.tensor.matmul_mx(
-                        out=qk[:, j, :],
+                        out=qk[:, tt, :],
                         lhsT=cod[:, col : col + P].bitcast(FP8X4),
                         lhsT_scale=scl[:, col : col + P],
                         rhs=wc_qk[:, 2 * D * g : 2 * D * (g + 1)].bitcast(FP8X4),
@@ -127,11 +127,11 @@ def tile_attention_pa_t_kernel(tc, x, rope, qkv_w, out_0, out_1, out_2):
                         start=(g == 0),
                         stop=(g == 1),
                     )
-            for tt in range(2 * h, 2 * h + 2):
+            for tt in range(R_T):
                 for g in range(2):
                     col = (2 * tt + g) * P
                     nc.tensor.matmul_mx(
-                        out=vbs[u][:, tt, :],
+                        out=vbs[r // 2][:, R_T * (r % 2) + tt, :],
                         lhsT=cod[:, col : col + P].bitcast(FP8X4),
                         lhsT_scale=scl[:, col : col + P],
                         rhs=wc_v[:, D * g : D * (g + 1)].bitcast(FP8X4),
@@ -140,80 +140,80 @@ def tile_attention_pa_t_kernel(tc, x, rope, qkv_w, out_0, out_1, out_2):
                         stop=(g == 1),
                     )
 
-        def v_out(u):
-            k, half, b, s = where(u)
-            if half == 0:
+        def v_out(m):
+            k, lt, b, s = where(2 * m)
+            if lt == 0:
                 vos[k] = vopool.tile([P, SU_T, D], F32, name="vo")
-            nc.scalar.copy(out=vos[k][:, U_T * half : U_T * (half + 1), :], in_=vbs[u][:])
+            nc.scalar.copy(out=vos[k][:, lt : lt + 2 * R_T, :], in_=vbs[m][:])
 
-        def products(u):
-            k, half, b, s = where(u)
-            if half == 0:
-                m1s[k] = m1pool.tile([P, 2, SU_T, D], F32, name="m1")
-            m2s[u] = m2pool.tile([P, 2, U_T, D], F32, name="m2")
-            shape = [P, 2, 2, D // 2, 2]
-            for h in range(2):
-                lt = U_T * half + 2 * h
-                t0 = SU_T * s + lt
-                pairs = qks[u][h][:].rearrange("p t (c j e) -> p t c j e", c=2, e=2)
-                for e, table, dst in (
-                    (0, rope_sb, m1s[k][:, :, lt : lt + 2, :]),
-                    (1, rope2, m2s[u][:, :, 2 * h : 2 * h + 2, :]),
-                ):
-                    nc.vector.tensor_tensor(
-                        out=dst.rearrange("p c t (j e) -> p t c j e", e=2),
-                        in0=pairs[:, :, :, :, e : e + 1].to_broadcast(shape),
-                        in1=table[:, t0 : t0 + 2, :].rearrange("p t (j e) -> p t j e", e=2).unsqueeze(2).to_broadcast(shape),
-                        op=ALU.mult,
-                    )
+        def products(r):
+            k, lt, b, s = where(r)
+            m1s[r] = m1pool.tile([P, 2, R_T, D], F32, name="m1")
+            m2s[r] = m2pool.tile([P, 2, R_T, D], F32, name="m2")
+            shape = [P, R_T, 2, D // 2, 2]
+            t0 = SU_T * s + lt
+            pairs = qks[r][:].rearrange("p t (c j e) -> p t c j e", c=2, e=2)
+            for e, table, dst in (
+                (0, rope_sb, m1s[r]),
+                (1, rope2, m2s[r]),
+            ):
+                nc.vector.tensor_tensor(
+                    out=dst[:].rearrange("p c t (j e) -> p t c j e", e=2),
+                    in0=pairs[:, :, :, :, e : e + 1].to_broadcast(shape),
+                    in1=table[:, t0 : t0 + R_T, :].rearrange("p t (j e) -> p t j e", e=2).unsqueeze(2).to_broadcast(shape),
+                    op=ALU.mult,
+                )
 
-        def add(u, h, engine):
-            k, half, b, s = where(u)
-            lt = U_T * half + 2 * h
-            dst = m1s[k][:, :, lt : lt + 2, :]
-            engine.tensor_tensor(out=dst, in0=dst, in1=m2s[u][:, :, 2 * h : 2 * h + 2, :], op=ALU.add)
+        def add(r, engine):
+            k, lt, b, s = where(r)
+            if lt == 0:
+                outs[k] = opool.tile([P, 2, SU_T, D], F32, name="out")
+            engine.tensor_tensor(out=outs[k][:, :, lt : lt + R_T, :], in0=m1s[r][:], in1=m2s[r][:], op=ALU.add)
 
         def stores(k):
             b, s = k % 2, k // 2
             rows = slice(SU_T * s, SU_T * (s + 1))
-            nc.sync.dma_start(out=o_v[0][b, :, rows, :], in_=m1s[k][:, 0, :, :])
-            nc.sync.dma_start(out=o_v[1][b, :, rows, :], in_=m1s[k][:, 1, :, :])
+            nc.sync.dma_start(out=o_v[0][b, :, rows, :], in_=outs[k][:, 0, :, :])
+            nc.sync.dma_start(out=o_v[1][b, :, rows, :], in_=outs[k][:, 1, :, :])
             nc.sync.dma_start(out=o_v[2][b, :, rows, :], in_=vos[k][:])
 
         make_identity(nc, ident[:])
-        load_x(0, 0, U_T)
+        load_x(0, 0, R_T)
         nc.sync.dma_start(
             out=wraw[:].rearrange("p g t c -> p g (t c)"),
             in_=qkv_w.rearrange("(g p t) c -> p g (t c)", p=P, t=4),
         )
+        load_x(0, R_T, SU_T)
         load_rope(0, SU_T)
-        load_x(0, U_T, SU_T)
         load_x(1, 0, SU_T)
         load_rope(SU_T, ROWS_PP)
         for k in range(2, NXS):
             load_x(k, 0, SU_T)
 
-        for i in range(N_U + 3):
-            for h in range(2):
-                if i < N_U:
-                    transposes(i, h)
-                    copies(i, h)
-                if 2 <= i < N_U + 2:
-                    mx(i - 2, h)
-            if i == 0:
-                prep_w()
-            if i < N_U:
-                quantise(i)
-            if i % 4 == 0 and i // 4 < ROWS_PP // SU_T:
-                prep_rope2(i // 4)
-            if i >= 3:
-                add(i - 3, 1, nc.vector)
-                if i % 2 == 0:
-                    k = (i - 3) // 2
-                    stores(k)
-                    if k + NXS < N_SU:
-                        load_x(k + NXS, 0, SU_T)
-            if 2 <= i < N_U + 2:
-                v_out(i - 2)
-                products(i - 2)
-                add(i - 2, 0, nc.gpsimd)
+        for m in range(N_R // 2 + 2):
+            new = [r for r in (2 * m, 2 * m + 1) if r < N_R]
+            old = [r for r in (2 * m - 2, 2 * m - 1) if 0 <= r < N_R]
+            for j in range(2):
+                if new:
+                    transposes(new[j])
+                    copies(new[j])
+                if m == 0 and j == 0:
+                    prep_w()
+                if new:
+                    quantise(new[j])
+                if old:
+                    mx(old[j])
+                if j == 0 and m >= 2:
+                    add(2 * m - 3, nc.vector)
+            if m % 4 == 0 and m // 4 < ROWS_PP // SU_T:
+                prep_rope2(m // 4)
+            if old:
+                v_out(m - 1)
+                products(old[0])
+                add(old[0], nc.gpsimd)
+                products(old[1])
+            if m >= 3 and m % 2 == 1:
+                k = (m - 3) // 2
+                stores(k)
+                if k + NXS < N_SU:
+                    load_x(k + NXS, 0, SU_T)

@@ -76,12 +76,11 @@ def tile_attention_pa_t_kernel(tc, x, rope, qkv_w, out_0, out_1, out_2):
             nc.scalar.activation(out=dst[:, :, :, 0:1], in_=src[:, :, :, 1:2], func=ACT.Copy, scale=-1.0)
             nc.scalar.copy(out=dst[:, :, :, 1:2], in_=src[:, :, :, 0:1])
 
-        def prep_w():
-            for g in range(2):
-                nc.vector.tensor_copy(out=wg_qk[:, g, :, :], in_=wraw[:, g, :, 0 : 2 * D].rearrange("p t c -> p c t"))
-            for g in range(2):
-                nc.vector.tensor_copy(out=wg_v[:, g, :, :], in_=wraw[:, g, :, 2 * D : 3 * D].rearrange("p t c -> p c t"))
+        def prep_w_and_first_pair():
+            nc.vector.tensor_copy(out=wg_qk[:], in_=wraw[:, :, :, 0 : 2 * D].rearrange("p g t c -> p g c t"))
+            quantise(0)
             nc.vector.quantize_mx(out=wc_qk[:].bitcast(FP8X4), scales=ws_qk[:], in_=wg_qk[:].rearrange("p g c t -> p (g c t)"))
+            nc.vector.tensor_copy(out=wg_v[:], in_=wraw[:, :, :, 2 * D : 3 * D].rearrange("p g t c -> p g c t"))
             nc.vector.quantize_mx(out=wc_v[:].bitcast(FP8X4), scales=ws_v[:], in_=wg_v[:].rearrange("p g c t -> p (g c t)"))
 
         def transposes(r):
@@ -170,12 +169,10 @@ def tile_attention_pa_t_kernel(tc, x, rope, qkv_w, out_0, out_1, out_2):
                 outs[k] = opool.tile([P, 2, SU_T, D], F32, name="out")
             engine.tensor_tensor(out=outs[k][:, :, lt : lt + R_T, :], in0=m1s[r][:], in1=m2s[r][:], op=ALU.add)
 
-        def stores(k):
+        def store(k, c, lo, hi):
             b, s = k % 2, k // 2
-            rows = slice(SU_T * s, SU_T * (s + 1))
-            nc.sync.dma_start(out=o_v[0][b, :, rows, :], in_=outs[k][:, 0, :, :])
-            nc.sync.dma_start(out=o_v[1][b, :, rows, :], in_=outs[k][:, 1, :, :])
-            nc.sync.dma_start(out=o_v[2][b, :, rows, :], in_=vos[k][:])
+            src = vos[k][:, lo:hi, :] if c == 2 else outs[k][:, c, lo:hi, :]
+            nc.sync.dma_start(out=o_v[c][b, :, SU_T * s + lo : SU_T * s + hi, :], in_=src)
 
         make_identity(nc, ident[:])
         load_x(0, 0, R_T)
@@ -183,37 +180,45 @@ def tile_attention_pa_t_kernel(tc, x, rope, qkv_w, out_0, out_1, out_2):
             out=wraw[:].rearrange("p g t c -> p g (t c)"),
             in_=qkv_w.rearrange("(g p t) c -> p g (t c)", p=P, t=4),
         )
-        load_x(0, R_T, SU_T)
+        load_x(0, R_T, 2 * R_T)
         load_rope(0, SU_T)
-        load_x(1, 0, SU_T)
+        load_x(0, 2 * R_T, SU_T)
+        load_x(1, 0, 2 * R_T)
+        load_x(1, 2 * R_T, SU_T)
         load_rope(SU_T, ROWS_PP)
         for k in range(2, NXS):
             load_x(k, 0, SU_T)
 
-        for m in range(N_R // 2 + 2):
+        for m in range(N_R // 2 + 1):
             new = [r for r in (2 * m, 2 * m + 1) if r < N_R]
             old = [r for r in (2 * m - 2, 2 * m - 1) if 0 <= r < N_R]
-            for j in range(2):
-                if new:
-                    transposes(new[j])
-                    copies(new[j])
-                if m == 0 and j == 0:
-                    prep_w()
-                if new:
-                    quantise(new[j])
-                if old:
-                    mx(old[j])
-                if j == 0 and m >= 2:
-                    add(2 * m - 3, nc.vector)
+            for r in new:
+                transposes(r)
+                copies(r)
+                if r == 0:
+                    prep_w_and_first_pair()
+                elif m != 1:
+                    quantise(r)
+            for r in old:
+                mx(r)
             if m % 4 == 0 and m // 4 < ROWS_PP // SU_T:
                 prep_rope2(m // 4)
             if old:
                 v_out(m - 1)
                 products(old[0])
                 add(old[0], nc.gpsimd)
+                if m == 1:
+                    quantise(new[0])
                 products(old[1])
-            if m >= 3 and m % 2 == 1:
-                k = (m - 3) // 2
-                stores(k)
-                if k + NXS < N_SU:
-                    load_x(k + NXS, 0, SU_T)
+                add(old[1], nc.gpsimd if new else nc.vector)
+                if m == 1:
+                    quantise(new[1])
+            if old:
+                k, lt, b, s = where(old[0])
+                ends = (lt, lt + 2 * R_T) if new else (lt, lt + R_T, lt + 2 * R_T)
+                store(k, 2, lt, lt + 2 * R_T)
+                for lo, hi in zip(ends[:-1], ends[1:]):
+                    store(k, 0, lo, hi)
+                    store(k, 1, lo, hi)
+            if m % 2 == 0 and m >= 2 and (m - 2) // 2 + NXS < N_SU:
+                load_x((m - 2) // 2 + NXS, 0, SU_T)

@@ -33,6 +33,7 @@ def tile_attention_pa_t_kernel(tc, x, rope, qkv_w, out_0, out_1, out_2):
     with ExitStack() as ctx:
         const = ctx.enter_context(tc.tile_pool(name="const", bufs=1))
         xpool = ctx.enter_context(tc.tile_pool(name="xpool", bufs=NXS))
+        xrpool = ctx.enter_context(tc.tile_pool(name="xrpool", bufs=2))
         gpool = ctx.enter_context(tc.tile_pool(name="gpool", bufs=4))
         cpool = ctx.enter_context(tc.tile_pool(name="cpool", bufs=5))
         opool = ctx.enter_context(tc.tile_pool(name="opool", bufs=3))
@@ -55,6 +56,7 @@ def tile_attention_pa_t_kernel(tc, x, rope, qkv_w, out_0, out_1, out_2):
         rope_sb = const.tile([P, ROWS_PP, D], BF16, name="rope_sb")
         rope2 = const.tile([P, ROWS_PP, D], BF16, name="rope2")
 
+        xrs = {}
         xs, tps, grps, cods, scls, qks, vbs, m1s, m2s, outs, vos = {}, {}, {}, {}, {}, {}, {}, {}, {}, {}, {}
 
         def where(r):
@@ -83,15 +85,27 @@ def tile_attention_pa_t_kernel(tc, x, rope, qkv_w, out_0, out_1, out_2):
             nc.vector.tensor_copy(out=wg_v[:], in_=wraw[:, :, :, 2 * D : 3 * D].rearrange("p g t c -> p g c t"))
             nc.vector.quantize_mx(out=wc_v[:].bitcast(FP8X4), scales=ws_v[:], in_=wg_v[:].rearrange("p g c t -> p (g c t)"))
 
+        def reorder(r, tt):
+            k, lt, b, s = where(r)
+            xr = xrpool.tile([P, HID], BF16, name="xr")
+            xrs[r, tt] = xr
+            nc.scalar.copy(
+                out=xr[:].bitcast(F32).rearrange("p (g w r) -> p g w r", g=2, w=2),
+                in_=xs[k][:, lt + tt, :].bitcast(F32).rearrange("p (g r w) -> p g w r", g=2, w=2),
+            )
+
         def transposes(r):
             k, lt, b, s = where(r)
             tps[r] = []
             for tt in range(R_T):
                 tp = tpool.tile([P, 4, P], F32, name="tp")
-                xf = xs[k][:, lt + tt, :].bitcast(F32)
                 for i in range(4):
-                    words = slice(2 * P * (i // 2) + i % 2, 2 * P * (i // 2 + 1), 2)
-                    nc.tensor.transpose(out=tp[:, i, :], in_=xf[:, words], identity=ident[:])
+                    if (r, tt) in xrs:
+                        words = xrs[r, tt][:].bitcast(F32)[:, P * i : P * (i + 1)]
+                    else:
+                        first = 2 * P * (i // 2) + i % 2
+                        words = xs[k][:, lt + tt, :].bitcast(F32)[:, first : 2 * P * (i // 2 + 1) : 2]
+                    nc.tensor.transpose(out=tp[:, i, :], in_=words, identity=ident[:])
                 tps[r].append(tp)
 
         def copies(r):
@@ -191,34 +205,32 @@ def tile_attention_pa_t_kernel(tc, x, rope, qkv_w, out_0, out_1, out_2):
 
         for m in range(N_R // 2 + 1):
             new = [r for r in (2 * m, 2 * m + 1) if r < N_R]
-            old = [r for r in (2 * m - 2, 2 * m - 1) if 0 <= r < N_R]
-            for r in new:
-                transposes(r)
-                copies(r)
-                if r == 0:
-                    prep_w_and_first_pair()
-                elif m != 1:
-                    quantise(r)
-            for r in old:
-                mx(r)
+            old = [r for r in (2 * m - 2, 2 * m - 1) if r >= 0]
+            for j in range(2):
+                if new:
+                    transposes(new[j])
+                    copies(new[j])
+                if j == 0 and m >= 2 and 2 * m + 3 < N_R:
+                    reorder(2 * m + 3, 0)
+                if old:
+                    mx(old[j])
             if m % 4 == 0 and m // 4 < ROWS_PP // SU_T:
                 prep_rope2(m // 4)
-            if old:
+            if m == 0:
+                prep_w_and_first_pair()
+                quantise(1)
+            else:
                 v_out(m - 1)
-                products(old[0])
-                add(old[0], nc.gpsimd)
-                if m == 1:
-                    quantise(new[0])
-                products(old[1])
-                add(old[1], nc.gpsimd if new else nc.vector)
-                if m == 1:
-                    quantise(new[1])
-            if old:
+                for j in range(2):
+                    products(old[j])
+                    add(old[j], nc.vector if old[j] == N_R - 1 else nc.gpsimd)
+                    if new:
+                        quantise(new[j])
                 k, lt, b, s = where(old[0])
                 ends = (lt, lt + 2 * R_T) if new else (lt, lt + R_T, lt + 2 * R_T)
                 store(k, 2, lt, lt + 2 * R_T)
                 for lo, hi in zip(ends[:-1], ends[1:]):
                     store(k, 0, lo, hi)
                     store(k, 1, lo, hi)
-            if m % 2 == 0 and m >= 2 and (m - 2) // 2 + NXS < N_SU:
-                load_x((m - 2) // 2 + NXS, 0, SU_T)
+                if m % 2 == 0 and (m - 2) // 2 + NXS < N_SU:
+                    load_x((m - 2) // 2 + NXS, 0, SU_T)

@@ -33,7 +33,7 @@ def tile_attention_pa_t_kernel(tc, x, rope, qkv_w, out_0, out_1, out_2):
     with ExitStack() as ctx:
         const = ctx.enter_context(tc.tile_pool(name="const", bufs=1))
         xpool = ctx.enter_context(tc.tile_pool(name="xpool", bufs=NXS))
-        xrpool = ctx.enter_context(tc.tile_pool(name="xrpool", bufs=2))
+        xrpool = ctx.enter_context(tc.tile_pool(name="xrpool", bufs=4))
         gpool = ctx.enter_context(tc.tile_pool(name="gpool", bufs=4))
         cpool = ctx.enter_context(tc.tile_pool(name="cpool", bufs=5))
         opool = ctx.enter_context(tc.tile_pool(name="opool", bufs=3))
@@ -85,11 +85,11 @@ def tile_attention_pa_t_kernel(tc, x, rope, qkv_w, out_0, out_1, out_2):
             nc.vector.tensor_copy(out=wg_v[:], in_=wraw[:, :, :, 2 * D : 3 * D].rearrange("p g t c -> p g c t"))
             nc.vector.quantize_mx(out=wc_v[:].bitcast(FP8X4), scales=ws_v[:], in_=wg_v[:].rearrange("p g c t -> p (g c t)"))
 
-        def reorder(r, tt):
+        def reorder(r, tt, copy):
             k, lt, b, s = where(r)
             xr = xrpool.tile([P, HID], BF16, name="xr")
             xrs[r, tt] = xr
-            nc.scalar.copy(
+            copy(
                 out=xr[:].bitcast(F32).rearrange("p (g w r) -> p g w r", g=2, w=2),
                 in_=xs[k][:, lt + tt, :].bitcast(F32).rearrange("p (g r w) -> p g w r", g=2, w=2),
             )
@@ -195,13 +195,14 @@ def tile_attention_pa_t_kernel(tc, x, rope, qkv_w, out_0, out_1, out_2):
             in_=qkv_w.rearrange("(g p t) c -> p g (t c)", p=P, t=4),
         )
         load_x(0, R_T, 2 * R_T)
+        load_x(0, 2 * R_T, 3 * R_T)
         load_rope(0, SU_T)
-        load_x(0, 2 * R_T, SU_T)
+        load_x(0, 3 * R_T, SU_T)
         load_x(1, 0, 2 * R_T)
         load_x(1, 2 * R_T, SU_T)
+        load_x(2, 0, SU_T)
         load_rope(SU_T, ROWS_PP)
-        for k in range(2, NXS):
-            load_x(k, 0, SU_T)
+        load_x(3, 0, SU_T)
 
         for m in range(N_R // 2 + 1):
             new = [r for r in (2 * m, 2 * m + 1) if r < N_R]
@@ -211,7 +212,7 @@ def tile_attention_pa_t_kernel(tc, x, rope, qkv_w, out_0, out_1, out_2):
                     transposes(new[j])
                     copies(new[j])
                 if j == 0 and m >= 2 and 2 * m + 3 < N_R:
-                    reorder(2 * m + 3, 0)
+                    reorder(2 * m + 3, 1, nc.scalar.copy)
                 if old:
                     mx(old[j])
             if m % 4 == 0 and m // 4 < ROWS_PP // SU_T:
@@ -226,6 +227,8 @@ def tile_attention_pa_t_kernel(tc, x, rope, qkv_w, out_0, out_1, out_2):
                     add(old[j], nc.vector if old[j] == N_R - 1 else nc.gpsimd)
                     if new:
                         quantise(new[j])
+                    if j == 0 and m >= 2 and 2 * m + 3 < N_R:
+                        reorder(2 * m + 3, 0, nc.vector.tensor_copy)
                 k, lt, b, s = where(old[0])
                 ends = (lt, lt + 2 * R_T) if new else (lt, lt + R_T, lt + 2 * R_T)
                 store(k, 2, lt, lt + 2 * R_T)

@@ -72,11 +72,13 @@ def tile_attention_pa_t_kernel(tc, x, rope, qkv_w, out_0, out_1, out_2):
         def load_rope(lo, hi):
             nc.sync.dma_start(out=rope_sb[:, lo:hi, :], in_=rope_v[:, lo:hi, :])
 
-        def prep_rope2(s):
-            src = rope_sb[:, SU_T * s : SU_T * (s + 1), :].rearrange("p t (j e) -> p t j e", e=2)
-            dst = rope2[:, SU_T * s : SU_T * (s + 1), :].rearrange("p t (j e) -> p t j e", e=2)
-            nc.scalar.activation(out=dst[:, :, :, 0:1], in_=src[:, :, :, 1:2], func=ACT.Copy, scale=-1.0)
-            nc.scalar.copy(out=dst[:, :, :, 1:2], in_=src[:, :, :, 0:1])
+        def prep_rope2(lo, hi, e):
+            src = rope_sb[:, lo:hi, :].rearrange("p t (j e) -> p t j e", e=2)[:, :, :, 1 - e : 2 - e]
+            dst = rope2[:, lo:hi, :].rearrange("p t (j e) -> p t j e", e=2)[:, :, :, e : e + 1]
+            if e == 0:
+                nc.scalar.activation(out=dst, in_=src, func=ACT.Copy, scale=-1.0)
+            else:
+                nc.scalar.copy(out=dst, in_=src)
 
         def prep_w_and_first_pair():
             nc.vector.tensor_copy(out=wg_qk[:], in_=wraw[:, :, :, 0 : 2 * D].rearrange("p g t c -> p g c t"))
@@ -199,9 +201,10 @@ def tile_attention_pa_t_kernel(tc, x, rope, qkv_w, out_0, out_1, out_2):
         load_rope(0, SU_T)
         load_x(0, 3 * R_T, SU_T)
         load_x(1, 0, 2 * R_T)
+        load_rope(SU_T, 2 * SU_T)
         load_x(1, 2 * R_T, SU_T)
         load_x(2, 0, SU_T)
-        load_rope(SU_T, ROWS_PP)
+        load_rope(2 * SU_T, ROWS_PP)
         load_x(3, 0, SU_T)
 
         for m in range(N_R // 2 + 1):
@@ -215,13 +218,16 @@ def tile_attention_pa_t_kernel(tc, x, rope, qkv_w, out_0, out_1, out_2):
                     reorder(2 * m + 3, 1, nc.scalar.copy)
                 if old:
                     mx(old[j])
-            if m % 4 == 0 and m // 4 < ROWS_PP // SU_T:
-                prep_rope2(m // 4)
             if m == 0:
+                for e in range(2):
+                    prep_rope2(0, SU_T, e)
                 prep_w_and_first_pair()
                 quantise(1)
             else:
                 v_out(m - 1)
+                lo = SU_T * ((m - 1) // 4 + 1) + (m - 1) % 4 // 2 * (SU_T // 2)
+                if lo < ROWS_PP:
+                    prep_rope2(lo, lo + SU_T // 2, (m - 1) % 2)
                 for j in range(2):
                     products(old[j])
                     add(old[j], nc.vector if old[j] == N_R - 1 else nc.gpsimd)

@@ -233,7 +233,7 @@ def tile_attention_pa_t_kernel(tc, x, rope, qkv_w, out_0, out_1, out_2):
                     add(old[j], nc.vector if old[j] == N_R - 1 else nc.gpsimd)
                     if new:
                         quantise(new[j])
-                    if j == 0 and m >= 2 and 2 * m + 3 < N_R:
+                    if j == 0 and m >= 2 and m % 2 == 0 and 2 * m + 3 < N_R:
                         reorder(2 * m + 3, 0, nc.vector.tensor_copy)
                 k, lt, b, s = where(old[0])
                 ends = (lt, lt + 2 * R_T) if new else (lt, lt + R_T, lt + 2 * R_T)

from contextlib import ExitStack

import concourse.mybir as mybir
from concourse.masks import make_identity

F32 = mybir.dt.float32
BF16 = mybir.dt.bfloat16
U32 = mybir.dt.uint32
U8 = mybir.dt.uint8
FP8X4 = mybir.dt.float8_e4m3fn_x4
ALU = mybir.AluOpType
ACT = mybir.ActivationFunctionType

P = 128
B, N, HID, D = 2, 4096, 1024, 128
FLOPS = 2 * B * N * HID * 3 * D

ROWS_PP = N // P
SU_T = 8
N_SU = B * ROWS_PP // SU_T
R_T = 2
N_R = N_SU * SU_T // R_T
R_SU = SU_T // R_T
NXS = 4


def tile_attention_pa_t_kernel(tc, x, rope, qkv_w, out_0, out_1, out_2):
    nc = tc.nc
    x_v = x.rearrange("b (p t) k -> b p t k", t=ROWS_PP)
    rope_v = rope.rearrange("(p t) o d -> p t (o d)", t=ROWS_PP)
    o_v = [o.rearrange("b h (p t) d -> (b h) p t d", t=ROWS_PP) for o in (out_0, out_1, out_2)]

    with ExitStack() as ctx:
        const = ctx.enter_context(tc.tile_pool(name="const", bufs=1))
        xpool = ctx.enter_context(tc.tile_pool(name="xpool", bufs=NXS))
        xrpool = ctx.enter_context(tc.tile_pool(name="xrpool", bufs=4))
        gpool = ctx.enter_context(tc.tile_pool(name="gpool", bufs=4))
        cpool = ctx.enter_context(tc.tile_pool(name="cpool", bufs=5))
        opool = ctx.enter_context(tc.tile_pool(name="opool", bufs=3))
        m1pool = ctx.enter_context(tc.tile_pool(name="m1pool", bufs=4))
        m2pool = ctx.enter_context(tc.tile_pool(name="m2pool", bufs=4))
        vopool = ctx.enter_context(tc.tile_pool(name="vopool", bufs=3))
        tpool = ctx.enter_context(tc.psum_pool(name="tpool", bufs=4))
        qkpool = ctx.enter_context(tc.psum_pool(name="qkpool", bufs=3))
        vpool = ctx.enter_context(tc.psum_pool(name="vpool", bufs=1))
        ctx.enter_context(tc.manual_schedule())

        ident = const.tile([P, P], F32, name="ident")
        wraw = const.tile([P, 2, 4, 3 * D], BF16, name="wraw")
        wg_qk = const.tile([P, 2, 2 * D, 4], BF16, name="wg_qk", align_bytes=64)
        wg_v = const.tile([P, 2, D, 4], BF16, name="wg_v", align_bytes=64)
        wc_qk = const.tile([P, 2 * 2 * D], U32, name="wc_qk", align_bytes=64)
        ws_qk = const.tile([P, 2 * 2 * D], U8, name="ws_qk", align_bytes=64)
        wc_v = const.tile([P, 2 * D], U32, name="wc_v", align_bytes=64)
        ws_v = const.tile([P, 2 * D], U8, name="ws_v", align_bytes=64)
        rope_sb = const.tile([P, ROWS_PP, D], BF16, name="rope_sb")
        rope2 = const.tile([P, ROWS_PP, D], BF16, name="rope2")

        xrs = {}
        xs, tps, grps, cods, scls, qks, vbs, m1s, m2s, outs, vos = {}, {}, {}, {}, {}, {}, {}, {}, {}, {}, {}

        def where(r):
            k = r // R_SU
            return k, R_T * (r % R_SU), k % 2, k // 2

        def load_x(k, lo, hi):
            if lo == 0:
                xs[k] = xpool.tile([P, SU_T, HID], BF16, name="xs")
            b, s = k % 2, k // 2
            nc.sync.dma_start(out=xs[k][:, lo:hi, :], in_=x_v[b, :, SU_T * s + lo : SU_T * s + hi, :])

        def load_rope(lo, hi):
            nc.sync.dma_start(out=rope_sb[:, lo:hi, :], in_=rope_v[:, lo:hi, :])

        def prep_rope2(lo, hi, e):
            src = rope_sb[:, lo:hi, :].rearrange("p t (j e) -> p t j e", e=2)[:, :, :, 1 - e : 2 - e]
            dst = rope2[:, lo:hi, :].rearrange("p t (j e) -> p t j e", e=2)[:, :, :, e : e + 1]
            if e == 0:
                nc.scalar.activation(out=dst, in_=src, func=ACT.Copy, scale=-1.0)
            else:
                nc.scalar.copy(out=dst, in_=src)

        def prep_w_and_first_pair():
            nc.vector.tensor_copy(out=wg_qk[:], in_=wraw[:, :, :, 0 : 2 * D].rearrange("p g t c -> p g c t"))
            quantise(0)
            nc.vector.quantize_mx(out=wc_qk[:].bitcast(FP8X4), scales=ws_qk[:], in_=wg_qk[:].rearrange("p g c t -> p (g c t)"))
            nc.vector.tensor_copy(out=wg_v[:], in_=wraw[:, :, :, 2 * D : 3 * D].rearrange("p g t c -> p g c t"))
            nc.vector.quantize_mx(out=wc_v[:].bitcast(FP8X4), scales=ws_v[:], in_=wg_v[:].rearrange("p g c t -> p (g c t)"))

        def reorder(r, tt, copy):
            k, lt, b, s = where(r)
            xr = xrpool.tile([P, HID], BF16, name="xr")
            xrs[r, tt] = xr
            copy(
                out=xr[:].bitcast(F32).rearrange("p (g w r) -> p g w r", g=2, w=2),
                in_=xs[k][:, lt + tt, :].bitcast(F32).rearrange("p (g r w) -> p g w r", g=2, w=2),
            )

        def transposes(r):
            k, lt, b, s = where(r)
            tps[r] = []
            for tt in range(R_T):
                tp = tpool.tile([P, 4, P], F32, name="tp")
                for i in range(4):
                    if (r, tt) in xrs:
                        words = xrs[r, tt][:].bitcast(F32)[:, P * i : P * (i + 1)]
                    else:
                        first = 2 * P * (i // 2) + i % 2
                        words = xs[k][:, lt + tt, :].bitcast(F32)[:, first : 2 * P * (i // 2 + 1) : 2]
                    nc.tensor.transpose(out=tp[:, i, :], in_=words, identity=ident[:])
                tps[r].append(tp)

        def copies(r):
            grps[r] = gpool.tile([P, R_T, HID], BF16, name="grp", align_bytes=64)
            for tt in range(R_T):
                nc.scalar.copy(
                    out=grps[r][:, tt, :].bitcast(F32).rearrange("p (g r w) -> p g r w", g=2, w=2),
                    in_=tps[r][tt][:].rearrange("p (g w) r -> p g r w", w=2),
                )

        def quantise(r):
            cod = cpool.tile([P, R_T * 2 * P], U32, name="cod", align_bytes=64)
            scl = cpool.tile([P, R_T * 2 * P], U8, name="scl", align_bytes=64)
            cods[r], scls[r] = cod, scl
            nc.vector.quantize_mx(out=cod[:].bitcast(FP8X4), scales=scl[:], in_=grps[r][:].rearrange("p t k -> p (t k)"))

        def mx(r):
            cod, scl = cods[r], scls[r]
            if r % 2 == 0:
                vbs[r // 2] = vpool.tile([P, 2 * R_T, D], F32, name="vb")
            qk = qkpool.tile([P, R_T, 2 * D], F32, name="qk")
            qks[r] = qk
            for tt in range(R_T):
                for g in range(2):
                    col = (2 * tt + g) * P
                    nc.tensor.matmul_mx(
                        out=qk[:, tt, :],
                        lhsT=cod[:, col : col + P].bitcast(FP8X4),
                        lhsT_scale=scl[:, col : col + P],
                        rhs=wc_qk[:, 2 * D * g : 2 * D * (g + 1)].bitcast(FP8X4),
                        rhs_scale=ws_qk[:, 2 * D * g : 2 * D * (g + 1)],
                        start=(g == 0),
                        stop=(g == 1),
                    )
            for tt in range(R_T):
                for g in range(2):
                    col = (2 * tt + g) * P
                    nc.tensor.matmul_mx(
                        out=vbs[r // 2][:, R_T * (r % 2) + tt, :],
                        lhsT=cod[:, col : col + P].bitcast(FP8X4),
                        lhsT_scale=scl[:, col : col + P],
                        rhs=wc_v[:, D * g : D * (g + 1)].bitcast(FP8X4),
                        rhs_scale=ws_v[:, D * g : D * (g + 1)],
                        start=(g == 0),
                        stop=(g == 1),
                    )

        def v_out(m):
            k, lt, b, s = where(2 * m)
            if lt == 0:
                vos[k] = vopool.tile([P, SU_T, D], F32, name="vo")
            nc.scalar.copy(out=vos[k][:, lt : lt + 2 * R_T, :], in_=vbs[m][:])

        def products(r):
            k, lt, b, s = where(r)
            m1s[r] = m1pool.tile([P, 2, R_T, D], F32, name="m1")
            m2s[r] = m2pool.tile([P, 2, R_T, D], F32, name="m2")
            shape = [P, R_T, 2, D // 2, 2]
            t0 = SU_T * s + lt
            pairs = qks[r][:].rearrange("p t (c j e) -> p t c j e", c=2, e=2)
            for e, table, dst in (
                (0, rope_sb, m1s[r]),
                (1, rope2, m2s[r]),
            ):
                nc.vector.tensor_tensor(
                    out=dst[:].rearrange("p c t (j e) -> p t c j e", e=2),
                    in0=pairs[:, :, :, :, e : e + 1].to_broadcast(shape),
                    in1=table[:, t0 : t0 + R_T, :].rearrange("p t (j e) -> p t j e", e=2).unsqueeze(2).to_broadcast(shape),
                    op=ALU.mult,
                )

        def add(r, engine):
            k, lt, b, s = where(r)
            if lt == 0:
                outs[k] = opool.tile([P, 2, SU_T, D], F32, name="out")
            engine.tensor_tensor(out=outs[k][:, :, lt : lt + R_T, :], in0=m1s[r][:], in1=m2s[r][:], op=ALU.add)

        def store(k, c, lo, hi):
            b, s = k % 2, k // 2
            src = vos[k][:, lo:hi, :] if c == 2 else outs[k][:, c, lo:hi, :]
            nc.sync.dma_start(out=o_v[c][b, :, SU_T * s + lo : SU_T * s + hi, :], in_=src)

        make_identity(nc, ident[:])
        load_x(0, 0, R_T)
        nc.sync.dma_start(
            out=wraw[:].rearrange("p g t c -> p g (t c)"),
            in_=qkv_w.rearrange("(g p t) c -> p g (t c)", p=P, t=4),
        )
        load_x(0, R_T, 2 * R_T)
        load_x(0, 2 * R_T, 3 * R_T)
        load_rope(0, SU_T)
        load_x(0, 3 * R_T, SU_T)
        load_x(1, 0, 2 * R_T)
        load_rope(SU_T, 2 * SU_T)
        load_x(1, 2 * R_T, SU_T)
        load_x(2, 0, SU_T)
        load_rope(2 * SU_T, ROWS_PP)
        load_x(3, 0, SU_T)

        for m in range(N_R // 2 + 1):
            new = [r for r in (2 * m, 2 * m + 1) if r < N_R]
            old = [r for r in (2 * m - 2, 2 * m - 1) if r >= 0]
            for j in range(2):
                if new:
                    transposes(new[j])
                    copies(new[j])
                if j == 0 and m >= 2 and 2 * m + 3 < N_R:
                    reorder(2 * m + 3, 1, nc.scalar.copy)
                if old:
                    mx(old[j])
            if m == 0:
                for e in range(2):
                    prep_rope2(0, SU_T, e)
                prep_w_and_first_pair()
                quantise(1)
            else:
                v_out(m - 1)
                lo = SU_T * ((m - 1) // 4 + 1) + (m - 1) % 4 // 2 * (SU_T // 2)
                if lo < ROWS_PP:
                    prep_rope2(lo, lo + SU_T // 2, (m - 1) % 2)
                for j in range(2):
                    products(old[j])
                    add(old[j], nc.vector if old[j] == N_R - 1 else nc.gpsimd)
                    if new:
                        quantise(new[j])
                    if j == 0 and m >= 2 and m % 2 == 0 and 2 * m + 3 < N_R:
                        reorder(2 * m + 3, 0, nc.vector.tensor_copy)
                k, lt, b, s = where(old[0])
                ends = (lt, lt + 2 * R_T) if new else (lt, lt + R_T, lt + 2 * R_T)
                store(k, 2, lt, lt + 2 * R_T)
                for lo, hi in zip(ends[:-1], ends[1:]):
                    store(k, 0, lo, hi)
                    store(k, 1, lo, hi)
                if m % 2 == 0 and (m - 2) // 2 + NXS < N_SU:
                    load_x((m - 2) // 2 + NXS, 0, SU_T)
